import numpy as np
import ml_dtypes


def mxq(x, axis, fmt="e4m3"):
    dtype, down = {"e4m3": (ml_dtypes.float8_e4m3fn, 7), "e5m2": (ml_dtypes.float8_e5m2, 14)}[fmt]
    v = np.moveaxis(np.asarray(x, np.float32).astype(ml_dtypes.bfloat16).astype(np.float64), axis, -1)
    blocks = v.reshape(v.shape[:-1] + (-1, 32))
    amax = np.abs(blocks).max(-1, keepdims=True)
    byte = np.maximum(np.where(amax > 0, np.frexp(amax)[1] - 1 + 127, 0) - down, 1)
    scale = np.exp2(byte - 127.0)
    codes = (blocks / scale).astype(np.float32).astype(dtype).astype(np.float64)
    return np.moveaxis((codes * scale).reshape(v.shape), -1, axis)


WIDE = False


def mx_kscale(k):
    if not WIDE:
        return np.ones(k)
    levels = np.array([10, -10, 5, -5, 0])
    a = np.random.permutation(np.resize(levels, k // 512 * 4)).reshape(k // 512, 4)
    idx = np.arange(k)
    return np.exp2(a[idx // 512, idx % 128 // 32])


BF16 = ml_dtypes.bfloat16


def bf(x):
    return np.asarray(x, np.float32).astype(BF16)


def f64(x):
    return np.asarray(x).astype(np.float64)


E2M1 = np.array([0.0, 0.5, 1.0, 1.5, 2.0, 3.0, 4.0, 6.0, -0.0, -0.5, -1.0, -1.5, -2.0, -3.0, -4.0, -6.0])


def pack_weight(w, fmt):
    k, n = w.shape
    w = f64(bf(w)).reshape(k // 32, 32, n)
    amax = np.abs(w).max(1)
    if fmt == "e4m3":
        byte = np.frexp(amax)[1] - 1 + 127 - 7
    else:
        mant, ex = np.frexp(amax / 6.0)
        byte = np.where(mant > 0.5, ex, ex - 1) + 127
    byte = np.clip(np.where(amax > 0, byte, 1), 1, 254)
    scaled = (w * np.exp2(127.0 - byte)[:, None, :]).reshape(k, n).astype(np.float32)
    by_word = np.ascontiguousarray(scaled.reshape(k // 512, 128, 4, n).transpose(0, 1, 3, 2))
    if fmt == "e4m3":
        words = by_word.astype(ml_dtypes.float8_e4m3fn).view(np.uint8)
    else:
        c = by_word.astype(ml_dtypes.float4_e2m1fn).view(np.uint8) & 0xF
        words = c[..., 0::2] | (c[..., 1::2] << 4)
    return np.ascontiguousarray(words), np.ascontiguousarray(byte.astype(np.uint8).reshape(k // 512, 16, n))


def unpack_weight(words, scales, fmt):
    g, p, n, _ = words.shape
    if fmt == "e4m3":
        vals = np.ascontiguousarray(words).view(ml_dtypes.float8_e4m3fn).astype(np.float64)
    else:
        nib = np.empty((g, p, n, 4), np.uint8)
        nib[..., 0::2] = words & 0xF
        nib[..., 1::2] = words >> 4
        vals = E2M1[nib]
    vals = vals * np.repeat(np.exp2(scales.astype(np.float64) - 127.0), 8, axis=1)[..., None]
    return vals.transpose(0, 1, 3, 2).reshape(g * 512, n)


B, N, G, L = 4096, 256, 128, 768
N2 = 2 * N
FMT = "e4m3"


def setup_inputs():
    s = mx_kscale(N2)
    Volt = bf(np.random.standard_normal((B, N2)) * s)
    Y = np.random.standard_normal((N2, N2)) / np.sqrt(N2) / s[None, :] / s[:, None]
    Yconj = np.random.standard_normal((N2, N2)) / np.sqrt(N2) / s[None, :] / s[:, None]
    Y_words, Y_scales = pack_weight(np.ascontiguousarray(Y.T), FMT)
    Yconj_words, Yconj_scales = pack_weight(np.ascontiguousarray(Yconj.T), FMT)
    return {
        "Volt": Volt,
        "Y_words": Y_words,
        "Y_scales": Y_scales,
        "Yconj_words": Yconj_words,
        "Yconj_scales": Yconj_scales,
    }


def reference(Volt, Y_words, Y_scales, Yconj_words, Yconj_scales):
    v = f64(Volt)
    vq = mxq(v, 1, "e4m3")
    quad_p = v * (vq @ unpack_weight(Y_words, Y_scales, FMT))
    quad_q = v * (vq @ unpack_weight(Yconj_words, Yconj_scales, FMT))
    return quad_p, quad_q

@@ -1,0 +1,132 @@
+import concourse.mybir as mybir
+from concourse.masks import make_identity
+
+F32 = mybir.dt.float32
+BF16 = mybir.dt.bfloat16
+I32 = mybir.dt.int32
+U32 = mybir.dt.uint32
+U8 = mybir.dt.uint8
+FP8X4 = mybir.dt.float8_e4m3fn_x4
+MULT = mybir.AluOpType.mult
+
+P = 128
+PACK = 4
+SAMPLES = 4096
+K = 512
+N = 512
+WEIGHTS = 2
+SAMPLE_TILES = SAMPLES // P
+CHUNK = 4
+CHUNKS = SAMPLE_TILES // CHUNK
+PAIRS = K // 2
+HALVES = 2
+TILES_PER_BANK = 2
+SCALE_ROWS = 4
+
+FLOPS = 2 * WEIGHTS * SAMPLES * K * N
+
+
+def tile_pinnlayer_pb_t_kernel(
+    tc, Volt, Y_words, Y_scales, Yconj_words, Yconj_scales, out_0, out_1
+):
+    nc = tc.nc
+    volt_rows = Volt.rearrange("(p s) k -> p s k", s=SAMPLE_TILES)
+    out_rows = [o.rearrange("(p s) n -> p s n", s=SAMPLE_TILES) for o in (out_0, out_1)]
+    weight_words = [Y_words, Yconj_words]
+    weight_scales = [Y_scales, Yconj_scales]
+
+    with (
+        tc.tile_pool(name="const", bufs=1) as const,
+        tc.tile_pool(name="volt", bufs=CHUNKS) as volt_pool,
+        tc.tile_pool(name="grouped", bufs=2) as grouped_pool,
+        tc.tile_pool(name="quantised", bufs=2) as quantised_pool,
+        tc.tile_pool(name="product", bufs=3) as product_pool,
+        tc.psum_pool(name="transposed", bufs=2) as transposed_pool,
+        tc.psum_pool(name="sums", bufs=6) as sums_pool,
+        tc.manual_schedule(),
+    ):
+        w_codes = []
+        w_scales = []
+        for w in range(WEIGHTS):
+            w_codes.append(const.tile([P, N], U32, name="w_codes_%d" % w, align_bytes=64))
+            w_scales.append(const.tile([P, N], U8, name="w_scales_%d" % w, align_bytes=64))
+            nc.vector.memset(w_scales[w][:].bitcast(I32), 0)
+
+        identity = const.tile([P, P], F32)
+        make_identity(nc, identity[:])
+
+        volt = [volt_pool.tile([P, CHUNK, K], BF16, name="volt", tag="volt") for c in range(CHUNKS)]
+
+        def load_volt(c):
+            nc.sync.dma_start(out=volt[c][:], in_=volt_rows[:, c * CHUNK : (c + 1) * CHUNK, :])
+
+        load_volt(0)
+        for w in range(WEIGHTS):
+            nc.sync.dma_start(
+                out=w_codes[w][:].bitcast(I32),
+                in_=weight_words[w][0].rearrange("p n t -> p (n t)").bitcast(I32),
+            )
+        for w in range(WEIGHTS):
+            for quadrant in range(P // 32):
+                nc.sync.dma_start(
+                    out=w_scales[w][32 * quadrant : 32 * quadrant + SCALE_ROWS, :].bitcast(I32),
+                    in_=weight_scales[w][
+                        0, SCALE_ROWS * quadrant : SCALE_ROWS * (quadrant + 1), :
+                    ].bitcast(I32),
+                )
+        for c in range(1, CHUNKS):
+            load_volt(c)
+
+        def transpose_chunk(c):
+            grouped = grouped_pool.tile([P, CHUNK, P, PACK], BF16, align_bytes=64)
+            for first in range(0, CHUNK, TILES_PER_BANK):
+                transposed = transposed_pool.tile([P, TILES_PER_BANK, HALVES, P], F32)
+                for j in range(TILES_PER_BANK):
+                    words = volt[c][:, first + j, :].bitcast(F32)
+                    for u in range(HALVES):
+                        nc.tensor.transpose(
+                            transposed[:, j, u, :], words[:, u:PAIRS:HALVES], identity[:]
+                        )
+                nc.scalar.copy(
+                    out=grouped[:, first : first + TILES_PER_BANK, :, :].bitcast(F32),
+                    in_=transposed[:].rearrange("p j u b -> p j b u"),
+                )
+            return grouped
+
+        def quantise_chunk(grouped):
+            codes = quantised_pool.tile([P, CHUNK * P], U32, align_bytes=64)
+            scales = quantised_pool.tile([P, CHUNK * P], U8, align_bytes=64)
+            nc.vector.quantize_mx(
+                out=codes[:].bitcast(FP8X4),
+                scales=scales[:],
+                in_=grouped[:].rearrange("p j b t -> p (j b t)"),
+            )
+            return codes, scales
+
+        def multiply_chunk(c, codes, scales, w):
+            product = product_pool.tile([P, CHUNK, N], F32, name="product_%d" % w)
+            for j in range(CHUNK):
+                samples = slice(j * P, (j + 1) * P)
+                sums = sums_pool.tile([P, N], F32)
+                nc.tensor.matmul_mx(
+                    out=sums[:],
+                    lhsT=codes[:, samples].bitcast(FP8X4),
+                    lhsT_scale=scales[:, samples],
+                    rhs=w_codes[w][:].bitcast(FP8X4),
+                    rhs_scale=w_scales[w][:],
+                    start=True,
+                    stop=True,
+                )
+                nc.vector.tensor_tensor(
+                    out=product[:, j, :], in0=sums[:], in1=volt[c][:, j, :], op=MULT
+                )
+            nc.sync.dma_start(
+                out=out_rows[w][:, c * CHUNK : (c + 1) * CHUNK, :], in_=product[:]
+            )
+
+        ready = quantise_chunk(transpose_chunk(0))
+        for c in range(CHUNKS):
+            multiply_chunk(c, ready[0], ready[1], 0)
+            following = quantise_chunk(transpose_chunk(c + 1)) if c + 1 < CHUNKS else None
+            multiply_chunk(c, ready[0], ready[1], 1)
+            ready = following

@@ -22,6 +22,7 @@ PAIRS = K // 2
 HALVES = 2
 TILES_PER_BANK = 2
 SCALE_ROWS = 4
+HELPED = 1
 
 FLOPS = 2 * WEIGHTS * SAMPLES * K * N
 
@@ -117,9 +118,15 @@ def tile_pinnlayer_pb_t_kernel(
                     start=True,
                     stop=True,
                 )
-                nc.vector.tensor_tensor(
-                    out=product[:, j, :], in0=sums[:], in1=volt[c][:, j, :], op=MULT
-                )
+                if j < HELPED:
+                    nc.scalar.copy(out=product[:, j, :], in_=sums[:])
+                    nc.gpsimd.tensor_tensor(
+                        out=product[:, j, :], in0=product[:, j, :], in1=volt[c][:, j, :], op=MULT
+                    )
+                else:
+                    nc.vector.tensor_tensor(
+                        out=product[:, j, :], in0=sums[:], in1=volt[c][:, j, :], op=MULT
+                    )
             nc.sync.dma_start(
                 out=out_rows[w][:, c * CHUNK : (c + 1) * CHUNK, :], in_=product[:]
             )

@@ -61,13 +61,12 @@ def tile_pinnlayer_pb_t_kernel(
         def load_volt(c):
             nc.sync.dma_start(out=volt[c][:], in_=volt_rows[:, c * CHUNK : (c + 1) * CHUNK, :])
 
-        load_volt(0)
         for w in range(WEIGHTS):
+            load_volt(w)
             nc.sync.dma_start(
                 out=w_codes[w][:].bitcast(I32),
                 in_=weight_words[w][0].rearrange("p n t -> p (n t)").bitcast(I32),
             )
-        for w in range(WEIGHTS):
             for quadrant in range(P // 32):
                 nc.sync.dma_start(
                     out=w_scales[w][32 * quadrant : 32 * quadrant + SCALE_ROWS, :].bitcast(I32),
@@ -75,7 +74,7 @@ def tile_pinnlayer_pb_t_kernel(
                         0, SCALE_ROWS * quadrant : SCALE_ROWS * (quadrant + 1), :
                     ].bitcast(I32),
                 )
-        for c in range(1, CHUNKS):
+        for c in range(WEIGHTS, CHUNKS):
             load_volt(c)
 
         def transpose_chunk(c):

@@ -22,6 +22,7 @@ PAIRS = K // 2
 HALVES = 2
 TILES_PER_BANK = 2
 SCALE_ROWS = 4
+LOADS = [[0], [1], [2, 3], [4, 5, 6, 7]]
 HELPED = 1
 
 FLOPS = 2 * WEIGHTS * SAMPLES * K * N
@@ -38,7 +39,7 @@ def tile_pinnlayer_pb_t_kernel(
 
     with (
         tc.tile_pool(name="const", bufs=1) as const,
-        tc.tile_pool(name="volt", bufs=CHUNKS) as volt_pool,
+        tc.tile_pool(name="volt", bufs=1) as volt_pool,
         tc.tile_pool(name="grouped", bufs=2) as grouped_pool,
         tc.tile_pool(name="quantised", bufs=2) as quantised_pool,
         tc.tile_pool(name="product", bufs=3) as product_pool,
@@ -56,13 +57,17 @@ def tile_pinnlayer_pb_t_kernel(
         identity = const.tile([P, P], F32)
         make_identity(nc, identity[:])
 
-        volt = [volt_pool.tile([P, CHUNK, K], BF16, name="volt", tag="volt") for c in range(CHUNKS)]
+        volt = {}
 
-        def load_volt(c):
-            nc.sync.dma_start(out=volt[c][:], in_=volt_rows[:, c * CHUNK : (c + 1) * CHUNK, :])
+        def load_volt(chunks):
+            loaded = volt_pool.tile([P, len(chunks) * CHUNK, K], BF16, name="volt_%d" % chunks[0])
+            nc.sync.dma_start(
+                out=loaded[:], in_=volt_rows[:, chunks[0] * CHUNK : (chunks[-1] + 1) * CHUNK, :]
+            )
+            for i, c in enumerate(chunks):
+                volt[c] = loaded[:, i * CHUNK : (i + 1) * CHUNK, :]
 
-        for w in range(WEIGHTS):
-            load_volt(w)
+        def load_weight(w):
             nc.sync.dma_start(
                 out=w_codes[w][:].bitcast(I32),
                 in_=weight_words[w][0].rearrange("p n t -> p (n t)").bitcast(I32),
@@ -74,8 +79,13 @@ def tile_pinnlayer_pb_t_kernel(
                         0, SCALE_ROWS * quadrant : SCALE_ROWS * (quadrant + 1), :
                     ].bitcast(I32),
                 )
-        for c in range(WEIGHTS, CHUNKS):
-            load_volt(c)
+
+        load_volt(LOADS[0])
+        load_weight(0)
+        load_volt(LOADS[1])
+        load_volt(LOADS[2])
+        load_weight(1)
+        load_volt(LOADS[3])
 
         def transpose_chunk(c):
             grouped = grouped_pool.tile([P, CHUNK, P, PACK], BF16, align_bytes=64)

@@ -24,6 +24,7 @@ TILES_PER_BANK = 2
 SCALE_ROWS = 4
 LOADS = [[0], [1], [2, 3], [4, 5, 6, 7]]
 HELPED = 1
+LAST_STORES = [2, 1, 1]
 
 FLOPS = 2 * WEIGHTS * SAMPLES * K * N
 
@@ -42,7 +43,7 @@ def tile_pinnlayer_pb_t_kernel(
         tc.tile_pool(name="volt", bufs=1) as volt_pool,
         tc.tile_pool(name="grouped", bufs=2) as grouped_pool,
         tc.tile_pool(name="quantised", bufs=2) as quantised_pool,
-        tc.tile_pool(name="product", bufs=3) as product_pool,
+        tc.tile_pool(name="product", bufs=5) as product_pool,
         tc.psum_pool(name="transposed", bufs=2) as transposed_pool,
         tc.psum_pool(name="sums", bufs=6) as sums_pool,
         tc.manual_schedule(),
@@ -114,31 +115,35 @@ def tile_pinnlayer_pb_t_kernel(
             return codes, scales
 
         def multiply_chunk(c, codes, scales, w):
-            product = product_pool.tile([P, CHUNK, N], F32, name="product_%d" % w)
-            for j in range(CHUNK):
-                samples = slice(j * P, (j + 1) * P)
-                sums = sums_pool.tile([P, N], F32)
-                nc.tensor.matmul_mx(
-                    out=sums[:],
-                    lhsT=codes[:, samples].bitcast(FP8X4),
-                    lhsT_scale=scales[:, samples],
-                    rhs=w_codes[w][:].bitcast(FP8X4),
-                    rhs_scale=w_scales[w][:],
-                    start=True,
-                    stop=True,
+            last_step = c == CHUNKS - 1 and w == WEIGHTS - 1
+            j = 0
+            for tiles in LAST_STORES if last_step else [CHUNK]:
+                product = product_pool.tile([P, tiles, N], F32, name="product_%d" % w)
+                for i in range(tiles):
+                    samples = slice(j * P, (j + 1) * P)
+                    sums = sums_pool.tile([P, N], F32)
+                    nc.tensor.matmul_mx(
+                        out=sums[:],
+                        lhsT=codes[:, samples].bitcast(FP8X4),
+                        lhsT_scale=scales[:, samples],
+                        rhs=w_codes[w][:].bitcast(FP8X4),
+                        rhs_scale=w_scales[w][:],
+                        start=True,
+                        stop=True,
+                    )
+                    if j < HELPED:
+                        nc.scalar.copy(out=product[:, i, :], in_=sums[:])
+                        nc.gpsimd.tensor_tensor(
+                            out=product[:, i, :], in0=product[:, i, :], in1=volt[c][:, j, :], op=MULT
+                        )
+                    else:
+                        nc.vector.tensor_tensor(
+                            out=product[:, i, :], in0=sums[:], in1=volt[c][:, j, :], op=MULT
+                        )
+                    j += 1
+                nc.sync.dma_start(
+                    out=out_rows[w][:, c * CHUNK + j - tiles : c * CHUNK + j, :], in_=product[:]
                 )
-                if j < HELPED:
-                    nc.scalar.copy(out=product[:, j, :], in_=sums[:])
-                    nc.gpsimd.tensor_tensor(
-                        out=product[:, j, :], in0=product[:, j, :], in1=volt[c][:, j, :], op=MULT
-                    )
-                else:
-                    nc.vector.tensor_tensor(
-                        out=product[:, j, :], in0=sums[:], in1=volt[c][:, j, :], op=MULT
-                    )
-            nc.sync.dma_start(
-                out=out_rows[w][:, c * CHUNK : (c + 1) * CHUNK, :], in_=product[:]
-            )
 
         ready = quantise_chunk(transpose_chunk(0))
         for c in range(CHUNKS):

@@ -104,14 +104,17 @@ def tile_pinnlayer_pb_t_kernel(
                 )
             return grouped
 
-        def quantise_chunk(grouped):
+        def quantise_chunk(grouped, parts):
             codes = quantised_pool.tile([P, CHUNK * P], U32, align_bytes=64)
             scales = quantised_pool.tile([P, CHUNK * P], U8, align_bytes=64)
-            nc.vector.quantize_mx(
-                out=codes[:].bitcast(FP8X4),
-                scales=scales[:],
-                in_=grouped[:].rearrange("p j b t -> p (j b t)"),
-            )
+            values = grouped[:].rearrange("p j b t -> p (j b t)")
+            width = CHUNK * P // parts
+            for first in range(0, CHUNK * P, width):
+                nc.vector.quantize_mx(
+                    out=codes[:, first : first + width].bitcast(FP8X4),
+                    scales=scales[:, first : first + width],
+                    in_=values[:, PACK * first : PACK * (first + width)],
+                )
             return codes, scales
 
         def multiply_chunk(c, codes, scales, w):
@@ -145,9 +148,9 @@ def tile_pinnlayer_pb_t_kernel(
                     out=out_rows[w][:, c * CHUNK + j - tiles : c * CHUNK + j, :], in_=product[:]
                 )
 
-        ready = quantise_chunk(transpose_chunk(0))
+        ready = quantise_chunk(transpose_chunk(0), 2)
         for c in range(CHUNKS):
             multiply_chunk(c, ready[0], ready[1], 0)
-            following = quantise_chunk(transpose_chunk(c + 1)) if c + 1 < CHUNKS else None
+            following = quantise_chunk(transpose_chunk(c + 1), 1) if c + 1 < CHUNKS else None
             multiply_chunk(c, ready[0], ready[1], 1)
             ready = following

@@ -20,11 +20,13 @@ CHUNK = 4
 CHUNKS = SAMPLE_TILES // CHUNK
 PAIRS = K // 2
 HALVES = 2
-TILES_PER_BANK = 2
+BANKS = 2
+FIRST_PARTS = 4
 SCALE_ROWS = 4
-LOADS = [[0], [1], [2, 3], [4, 5, 6, 7]]
+LOADS = [2, 2, 8, 20]
 HELPED = 1
 LAST_STORES = [2, 1, 1]
+WARM_UP = 7
 
 FLOPS = 2 * WEIGHTS * SAMPLES * K * N
 
@@ -55,18 +57,22 @@ def tile_pinnlayer_pb_t_kernel(
             w_scales.append(const.tile([P, N], U8, name="w_scales_%d" % w, align_bytes=64))
             nc.vector.memset(w_scales[w][:].bitcast(I32), 0)
 
+        zeros = const.tile([P, N], BF16)
+        nc.gpsimd.memset(zeros[:], 0.0)
+        idle_sums = sums_pool.tile([P, N], F32, name="sums")
+        for i in range(WARM_UP):
+            nc.tensor.matmul(out=idle_sums[:], lhsT=zeros[:, :P], rhs=zeros[:], start=True, stop=True)
+
         identity = const.tile([P, P], F32)
         make_identity(nc, identity[:])
 
-        volt = {}
+        volt = []
 
-        def load_volt(chunks):
-            loaded = volt_pool.tile([P, len(chunks) * CHUNK, K], BF16, name="volt_%d" % chunks[0])
-            nc.sync.dma_start(
-                out=loaded[:], in_=volt_rows[:, chunks[0] * CHUNK : (chunks[-1] + 1) * CHUNK, :]
-            )
-            for i, c in enumerate(chunks):
-                volt[c] = loaded[:, i * CHUNK : (i + 1) * CHUNK, :]
+        def load_volt(tiles):
+            first = len(volt)
+            loaded = volt_pool.tile([P, tiles, K], BF16, name="volt_%d" % first)
+            nc.sync.dma_start(out=loaded[:], in_=volt_rows[:, first : first + tiles, :])
+            volt.extend([loaded[:, i, :] for i in range(tiles)])
 
         def load_weight(w):
             nc.sync.dma_start(
@@ -82,24 +88,25 @@ def tile_pinnlayer_pb_t_kernel(
                 )
 
         load_volt(LOADS[0])
-        load_weight(0)
         load_volt(LOADS[1])
+        load_weight(0)
         load_volt(LOADS[2])
         load_weight(1)
         load_volt(LOADS[3])
 
-        def transpose_chunk(c):
+        def transpose_chunk(c, parts):
             grouped = grouped_pool.tile([P, CHUNK, P, PACK], BF16, align_bytes=64)
-            for first in range(0, CHUNK, TILES_PER_BANK):
-                transposed = transposed_pool.tile([P, TILES_PER_BANK, HALVES, P], F32)
-                for j in range(TILES_PER_BANK):
-                    words = volt[c][:, first + j, :].bitcast(F32)
+            tiles = CHUNK // parts
+            for first in range(0, CHUNK, tiles):
+                transposed = transposed_pool.tile([P, tiles, HALVES, P], F32)
+                for j in range(tiles):
+                    words = volt[c * CHUNK + first + j].bitcast(F32)
                     for u in range(HALVES):
                         nc.tensor.transpose(
                             transposed[:, j, u, :], words[:, u:PAIRS:HALVES], identity[:]
                         )
                 nc.scalar.copy(
-                    out=grouped[:, first : first + TILES_PER_BANK, :, :].bitcast(F32),
+                    out=grouped[:, first : first + tiles, :, :].bitcast(F32),
                     in_=transposed[:].rearrange("p j u b -> p j b u"),
                 )
             return grouped
@@ -137,20 +144,20 @@ def tile_pinnlayer_pb_t_kernel(
                     if j < HELPED:
                         nc.scalar.copy(out=product[:, i, :], in_=sums[:])
                         nc.gpsimd.tensor_tensor(
-                            out=product[:, i, :], in0=product[:, i, :], in1=volt[c][:, j, :], op=MULT
+                            out=product[:, i, :], in0=product[:, i, :], in1=volt[c * CHUNK + j], op=MULT
                         )
                     else:
                         nc.vector.tensor_tensor(
-                            out=product[:, i, :], in0=sums[:], in1=volt[c][:, j, :], op=MULT
+                            out=product[:, i, :], in0=sums[:], in1=volt[c * CHUNK + j], op=MULT
                         )
                     j += 1
                 nc.sync.dma_start(
                     out=out_rows[w][:, c * CHUNK + j - tiles : c * CHUNK + j, :], in_=product[:]
                 )
 
-        ready = quantise_chunk(transpose_chunk(0), 2)
+        ready = quantise_chunk(transpose_chunk(0, FIRST_PARTS), FIRST_PARTS)
         for c in range(CHUNKS):
             multiply_chunk(c, ready[0], ready[1], 0)
-            following = quantise_chunk(transpose_chunk(c + 1), 1) if c + 1 < CHUNKS else None
+            following = quantise_chunk(transpose_chunk(c + 1, BANKS), 1) if c + 1 < CHUNKS else None
             multiply_chunk(c, ready[0], ready[1], 1)
             ready = following

@@ -26,7 +26,7 @@ SCALE_ROWS = 4
 LOADS = [2, 2, 8, 20]
 HELPED = 1
 LAST_STORES = [2, 1, 1]
-WARM_UP = 7
+WARM_UP = 4
 
 FLOPS = 2 * WEIGHTS * SAMPLES * K * N
 
@@ -50,18 +50,18 @@ def tile_pinnlayer_pb_t_kernel(
         tc.psum_pool(name="sums", bufs=6) as sums_pool,
         tc.manual_schedule(),
     ):
+        zeros = const.tile([P, N], BF16)
+        nc.vector.memset(zeros[:].bitcast(I32), 0)
+        idle_sums = sums_pool.tile([P, N], F32, name="sums")
+        for i in range(WARM_UP):
+            nc.tensor.matmul(out=idle_sums[:], lhsT=zeros[:, :P], rhs=zeros[:], start=True, stop=True)
+
         w_codes = []
         w_scales = []
         for w in range(WEIGHTS):
             w_codes.append(const.tile([P, N], U32, name="w_codes_%d" % w, align_bytes=64))
             w_scales.append(const.tile([P, N], U8, name="w_scales_%d" % w, align_bytes=64))
             nc.vector.memset(w_scales[w][:].bitcast(I32), 0)
-
-        zeros = const.tile([P, N], BF16)
-        nc.gpsimd.memset(zeros[:], 0.0)
-        idle_sums = sums_pool.tile([P, N], F32, name="sums")
-        for i in range(WARM_UP):
-            nc.tensor.matmul(out=idle_sums[:], lhsT=zeros[:, :P], rhs=zeros[:], start=True, stop=True)
 
         identity = const.tile([P, P], F32)
         make_identity(nc, identity[:])

@@ -26,6 +26,7 @@ SCALE_ROWS = 4
 LOADS = [2, 2, 8, 20]
 HELPED = 1
 LAST_STORES = [2, 1, 1]
+DMA_ALIGN = 256
 WARM_UP = 4
 
 FLOPS = 2 * WEIGHTS * SAMPLES * K * N
@@ -59,8 +60,8 @@ def tile_pinnlayer_pb_t_kernel(
         w_codes = []
         w_scales = []
         for w in range(WEIGHTS):
-            w_codes.append(const.tile([P, N], U32, name="w_codes_%d" % w, align_bytes=64))
-            w_scales.append(const.tile([P, N], U8, name="w_scales_%d" % w, align_bytes=64))
+            w_codes.append(const.tile([P, N], U32, name="w_codes_%d" % w, align_bytes=DMA_ALIGN))
+            w_scales.append(const.tile([P, N], U8, name="w_scales_%d" % w, align_bytes=DMA_ALIGN))
             nc.vector.memset(w_scales[w][:].bitcast(I32), 0)
 
         identity = const.tile([P, P], F32)
@@ -70,7 +71,7 @@ def tile_pinnlayer_pb_t_kernel(
 
         def load_volt(tiles):
             first = len(volt)
-            loaded = volt_pool.tile([P, tiles, K], BF16, name="volt_%d" % first)
+            loaded = volt_pool.tile([P, tiles, K], BF16, name="volt_%d" % first, align_bytes=DMA_ALIGN)
             nc.sync.dma_start(out=loaded[:], in_=volt_rows[:, first : first + tiles, :])
             volt.extend([loaded[:, i, :] for i in range(tiles)])
 
@@ -128,7 +129,9 @@ def tile_pinnlayer_pb_t_kernel(
             last_step = c == CHUNKS - 1 and w == WEIGHTS - 1
             j = 0
             for tiles in LAST_STORES if last_step else [CHUNK]:
-                product = product_pool.tile([P, tiles, N], F32, name="product_%d" % w)
+                product = product_pool.tile(
+                    [P, tiles, N], F32, name="product_%d" % w, align_bytes=DMA_ALIGN
+                )
                 for i in range(tiles):
                     samples = slice(j * P, (j + 1) * P)
                     sums = sums_pool.tile([P, N], F32)

import concourse.mybir as mybir
from concourse.masks import make_identity

F32 = mybir.dt.float32
BF16 = mybir.dt.bfloat16
I32 = mybir.dt.int32
U32 = mybir.dt.uint32
U8 = mybir.dt.uint8
FP8X4 = mybir.dt.float8_e4m3fn_x4
MULT = mybir.AluOpType.mult

P = 128
PACK = 4
SAMPLES = 4096
K = 512
N = 512
WEIGHTS = 2
SAMPLE_TILES = SAMPLES // P
CHUNK = 4
CHUNKS = SAMPLE_TILES // CHUNK
PAIRS = K // 2
HALVES = 2
BANKS = 2
FIRST_PARTS = 4
SCALE_ROWS = 4
LOADS = [2, 2, 8, 20]
HELPED = 1
LAST_STORES = [2, 1, 1]
DMA_ALIGN = 256
WARM_UP = 4

FLOPS = 2 * WEIGHTS * SAMPLES * K * N


def tile_pinnlayer_pb_t_kernel(
    tc, Volt, Y_words, Y_scales, Yconj_words, Yconj_scales, out_0, out_1
):
    nc = tc.nc
    volt_rows = Volt.rearrange("(p s) k -> p s k", s=SAMPLE_TILES)
    out_rows = [o.rearrange("(p s) n -> p s n", s=SAMPLE_TILES) for o in (out_0, out_1)]
    weight_words = [Y_words, Yconj_words]
    weight_scales = [Y_scales, Yconj_scales]

    with (
        tc.tile_pool(name="const", bufs=1) as const,
        tc.tile_pool(name="volt", bufs=1) as volt_pool,
        tc.tile_pool(name="grouped", bufs=2) as grouped_pool,
        tc.tile_pool(name="quantised", bufs=2) as quantised_pool,
        tc.tile_pool(name="product", bufs=5) as product_pool,
        tc.psum_pool(name="transposed", bufs=2) as transposed_pool,
        tc.psum_pool(name="sums", bufs=6) as sums_pool,
        tc.manual_schedule(),
    ):
        zeros = const.tile([P, N], BF16)
        nc.vector.memset(zeros[:].bitcast(I32), 0)
        idle_sums = sums_pool.tile([P, N], F32, name="sums")
        for i in range(WARM_UP):
            nc.tensor.matmul(out=idle_sums[:], lhsT=zeros[:, :P], rhs=zeros[:], start=True, stop=True)

        w_codes = []
        w_scales = []
        for w in range(WEIGHTS):
            w_codes.append(const.tile([P, N], U32, name="w_codes_%d" % w, align_bytes=DMA_ALIGN))
            w_scales.append(const.tile([P, N], U8, name="w_scales_%d" % w, align_bytes=DMA_ALIGN))
            nc.vector.memset(w_scales[w][:].bitcast(I32), 0)

        identity = const.tile([P, P], F32)
        make_identity(nc, identity[:])

        volt = []

        def load_volt(tiles):
            first = len(volt)
            loaded = volt_pool.tile([P, tiles, K], BF16, name="volt_%d" % first, align_bytes=DMA_ALIGN)
            nc.sync.dma_start(out=loaded[:], in_=volt_rows[:, first : first + tiles, :])
            volt.extend([loaded[:, i, :] for i in range(tiles)])

        def load_weight(w):
            nc.sync.dma_start(
                out=w_codes[w][:].bitcast(I32),
                in_=weight_words[w][0].rearrange("p n t -> p (n t)").bitcast(I32),
            )
            for quadrant in range(P // 32):
                nc.sync.dma_start(
                    out=w_scales[w][32 * quadrant : 32 * quadrant + SCALE_ROWS, :].bitcast(I32),
                    in_=weight_scales[w][
                        0, SCALE_ROWS * quadrant : SCALE_ROWS * (quadrant + 1), :
                    ].bitcast(I32),
                )

        load_volt(LOADS[0])
        load_volt(LOADS[1])
        load_weight(0)
        load_volt(LOADS[2])
        load_weight(1)
        load_volt(LOADS[3])

        def transpose_chunk(c, parts):
            grouped = grouped_pool.tile([P, CHUNK, P, PACK], BF16, align_bytes=64)
            tiles = CHUNK // parts
            for first in range(0, CHUNK, tiles):
                transposed = transposed_pool.tile([P, tiles, HALVES, P], F32)
                for j in range(tiles):
                    words = volt[c * CHUNK + first + j].bitcast(F32)
                    for u in range(HALVES):
                        nc.tensor.transpose(
                            transposed[:, j, u, :], words[:, u:PAIRS:HALVES], identity[:]
                        )
                nc.scalar.copy(
                    out=grouped[:, first : first + tiles, :, :].bitcast(F32),
                    in_=transposed[:].rearrange("p j u b -> p j b u"),
                )
            return grouped

        def quantise_chunk(grouped, parts):
            codes = quantised_pool.tile([P, CHUNK * P], U32, align_bytes=64)
            scales = quantised_pool.tile([P, CHUNK * P], U8, align_bytes=64)
            values = grouped[:].rearrange("p j b t -> p (j b t)")
            width = CHUNK * P // parts
            for first in range(0, CHUNK * P, width):
                nc.vector.quantize_mx(
                    out=codes[:, first : first + width].bitcast(FP8X4),
                    scales=scales[:, first : first + width],
                    in_=values[:, PACK * first : PACK * (first + width)],
                )
            return codes, scales

        def multiply_chunk(c, codes, scales, w):
            last_step = c == CHUNKS - 1 and w == WEIGHTS - 1
            j = 0
            for tiles in LAST_STORES if last_step else [CHUNK]:
                product = product_pool.tile(
                    [P, tiles, N], F32, name="product_%d" % w, align_bytes=DMA_ALIGN
                )
                for i in range(tiles):
                    samples = slice(j * P, (j + 1) * P)
                    sums = sums_pool.tile([P, N], F32)
                    nc.tensor.matmul_mx(
                        out=sums[:],
                        lhsT=codes[:, samples].bitcast(FP8X4),
                        lhsT_scale=scales[:, samples],
                        rhs=w_codes[w][:].bitcast(FP8X4),
                        rhs_scale=w_scales[w][:],
                        start=True,
                        stop=True,
                    )
                    if j < HELPED:
                        nc.scalar.copy(out=product[:, i, :], in_=sums[:])
                        nc.gpsimd.tensor_tensor(
                            out=product[:, i, :], in0=product[:, i, :], in1=volt[c * CHUNK + j], op=MULT
                        )
                    else:
                        nc.vector.tensor_tensor(
                            out=product[:, i, :], in0=sums[:], in1=volt[c * CHUNK + j], op=MULT
                        )
                    j += 1
                nc.sync.dma_start(
                    out=out_rows[w][:, c * CHUNK + j - tiles : c * CHUNK + j, :], in_=product[:]
                )

        ready = quantise_chunk(transpose_chunk(0, FIRST_PARTS), FIRST_PARTS)
        for c in range(CHUNKS):
            multiply_chunk(c, ready[0], ready[1], 0)
            following = quantise_chunk(transpose_chunk(c + 1, BANKS), 1) if c + 1 < CHUNKS else None
            multiply_chunk(c, ready[0], ready[1], 1)
            ready = following
